import numpy as np
import ml_dtypes


def mxq(x, axis, fmt="e4m3"):
    dtype, down = {"e4m3": (ml_dtypes.float8_e4m3fn, 7), "e5m2": (ml_dtypes.float8_e5m2, 14)}[fmt]
    v = np.moveaxis(np.asarray(x, np.float32).astype(ml_dtypes.bfloat16).astype(np.float64), axis, -1)
    blocks = v.reshape(v.shape[:-1] + (-1, 32))
    amax = np.abs(blocks).max(-1, keepdims=True)
    byte = np.maximum(np.where(amax > 0, np.frexp(amax)[1] - 1 + 127, 0) - down, 1)
    scale = np.exp2(byte - 127.0)
    codes = (blocks / scale).astype(np.float32).astype(dtype).astype(np.float64)
    return np.moveaxis((codes * scale).reshape(v.shape), -1, axis)


WIDE = False


def mx_kscale(k):
    if not WIDE:
        return np.ones(k)
    levels = np.array([10, -10, 5, -5, 0])
    a = np.random.permutation(np.resize(levels, k // 512 * 4)).reshape(k // 512, 4)
    idx = np.arange(k)
    return np.exp2(a[idx // 512, idx % 128 // 32])


BF16 = ml_dtypes.bfloat16


def bf(x):
    return np.asarray(x, np.float32).astype(BF16)


def f64(x):
    return np.asarray(x).astype(np.float64)


B, L, H, U = 2, 1024, 1024, 1024
R_MIN, R_MAX = 0.9, 0.999


def setup_inputs():
    s, t = mx_kscale(H), mx_kscale(U)
    inputs = np.random.standard_normal((B, L, H)) * s
    Wi = np.random.standard_normal((U, H)) / np.sqrt(H) / s[None, :] * t[:, None]
    bi = np.random.standard_normal(U) * 0.03 * t
    Wo = np.random.standard_normal((H, U)) / np.sqrt(U) / t[None, :]
    bo = np.random.standard_normal(H) * 0.1
    r = np.random.uniform(size=U)
    nu_log = np.log(-0.5 * np.log(r * (R_MAX ** 2 - R_MIN ** 2) + R_MIN ** 2))
    gamma_log = np.log(np.sqrt(1.0 - np.exp(-np.exp(nu_log)) ** 2))
    params_log = np.stack([nu_log, gamma_log])
    return {"inputs": bf(inputs), "Wi": bf(Wi), "bi": bf(bi), "Wo": bf(Wo), "bo": bf(bo), "params_log": bf(params_log)}


def reference(inputs, Wi, bi, Wo, bo, params_log):
    u = (mxq(f64(inputs), 2, "e4m3") @ mxq(f64(Wi), 1, "e4m3").T) + f64(bi)
    params = np.exp(f64(params_log))
    nu, gamma = params[0], params[1]

    log2_L = int(np.ceil(np.log2(L)))
    pad_len = 2 ** log2_L - L
    x = np.pad(u, ((0, 0), (0, pad_len), (0, 0))) if pad_len else u
    Lp = 2 ** log2_L

    for i in range(1, log2_L + 1):
        l = 2 ** i
        x = x.reshape(B * Lp // l, l, U)
        x1, x2 = x[:, : l // 2], x[:, l // 2:]
        pos = np.arange(1, l // 2 + 1, dtype=np.float64)
        lambs = np.exp(-pos[:, None] * nu)
        x2 = x2 + lambs * x1[:, -1:]
        x = np.concatenate([x1, x2], axis=1).reshape(B, Lp, U)

    x = x[:, :L] * gamma
    return (mxq(x, 2, "e4m3") @ mxq(f64(Wo), 1, "e4m3").T) + f64(bo)

@@ -1,0 +1,246 @@
+from contextlib import ExitStack
+
+import concourse.bass as bass
+import concourse.mybir as mybir
+import concourse.tile as tile
+from concourse.masks import make_identity
+
+F32 = mybir.dt.float32
+BF16 = mybir.dt.bfloat16
+U32 = mybir.dt.uint32
+U8 = mybir.dt.uint8
+FP8X4 = mybir.dt.float8_e4m3fn_x4
+ACTF = mybir.ActivationFunctionType
+ALU = mybir.AluOpType
+
+P = 128
+TOK = 2048
+SEQ = 1024
+H = 1024
+U = 1024
+CH = 512
+NCH = TOK // CH
+
+FLOPS = 2 * 2 * TOK * H * U
+
+
+def tile_slru_kernel(tc, inputs, Wi, bi, Wo, bo, params_log, out):
+    nc = tc.nc
+    x_in = inputs.flatten_outer_dims()
+    o_out = out.flatten_outer_dims()
+    with ExitStack() as ctx:
+        const = ctx.enter_context(tc.tile_pool(name="const", bufs=1))
+        rawp = ctx.enter_context(tc.tile_pool(name="raw", bufs=1))
+        keep = ctx.enter_context(tc.tile_pool(name="keep", bufs=1))
+        stg = ctx.enter_context(tc.tile_pool(name="stg", bufs=2))
+        vpool = ctx.enter_context(tc.tile_pool(name="vp", bufs=8))
+        xpool = ctx.enter_context(tc.tile_pool(name="xp", bufs=4))
+        gpool = ctx.enter_context(tc.tile_pool(name="gp", bufs=2))
+        opool = ctx.enter_context(tc.tile_pool(name="op", bufs=4))
+        ps_t = ctx.enter_context(tc.psum_pool(name="pst", bufs=2))
+        ps_1 = ctx.enter_context(tc.psum_pool(name="ps1", bufs=3))
+        ps_2 = ctx.enter_context(tc.psum_pool(name="ps2", bufs=3))
+
+        in_raw = []
+        for c in range(NCH):
+            t = rawp.tile([P, 4, H], BF16, name="in_raw%d" % c)
+            in_raw.append(t)
+        wi_raw = []
+        for a in range(4):
+            t = rawp.tile([P, 2, H], BF16, name="wi_raw%d" % a)
+            wi_raw.append(t)
+        wo_raw = []
+        for h in range(2):
+            t = rawp.tile([P, 4, U], BF16, name="wo_raw%d" % h)
+            wo_raw.append(t)
+
+        pl = [const.tile([P, 8], BF16, name="pl%d" % r) for r in range(2)]
+        bi_b = const.tile([P, 8], BF16, name="bi_b")
+        for r in range(2):
+            nc.scalar.dma_start(
+                out=pl[r][:].rearrange("m (a e) -> m a e", e=2),
+                in_=params_log[r].rearrange("(a m e) -> m a e", a=4, e=2),
+            )
+        nc.scalar.dma_start(
+            out=bi_b[:].rearrange("m (a e) -> m a e", e=2),
+            in_=bi.rearrange("(a m e) -> m a e", a=4, e=2),
+        )
+
+        def load_in(c, split):
+            src = x_in[c * CH : (c + 1) * CH, :].rearrange("(i p) h -> p i h", p=P)
+            if split:
+                for i in range(4):
+                    nc.sync.dma_start(out=in_raw[c][:, i, :], in_=src[:, i, :])
+            else:
+                nc.sync.dma_start(out=in_raw[c][:], in_=src)
+
+        def load_wi(a):
+            nc.sync.dma_start(
+                out=wi_raw[a][:],
+                in_=Wi[a * 256 : (a + 1) * 256, :].rearrange("(m e) h -> m e h", e=2),
+            )
+
+        def load_wo(h):
+            nc.sync.dma_start(
+                out=wo_raw[h][:],
+                in_=Wo[h * 512 : (h + 1) * 512, :].rearrange("(i p) u -> p i u", p=P),
+            )
+
+        load_in(0, True)
+        for a in range(4):
+            load_wi(a)
+        load_in(1, False)
+        load_wo(0)
+        load_wo(1)
+        load_in(2, False)
+        load_in(3, False)
+
+        bo_b = const.tile([P, H], BF16, name="bo_b")
+        nc.gpsimd.dma_start(out=bo_b[:], in_=bo.partition_broadcast(P))
+
+        ident = const.tile([P, P], F32, name="ident")
+        make_identity(nc, ident[:])
+
+        nu = const.tile([P, 8], F32, name="nu")
+        lam = const.tile([P, 8], F32, name="lam")
+        gam = const.tile([P, 8], F32, name="gam")
+        gb = const.tile([P, 8], F32, name="gb")
+        bi_f = const.tile([P, 8], F32, name="bi_f")
+        nc.scalar.activation(out=nu[:], in_=pl[0][:], func=ACTF.Exp)
+        nc.scalar.activation(out=lam[:], in_=nu[:], func=ACTF.Exp, scale=-1.0)
+        nc.scalar.activation(out=gam[:], in_=pl[1][:], func=ACTF.Exp)
+        nc.vector.tensor_copy(out=bi_f[:], in_=bi_b[:])
+        nc.vector.tensor_tensor(out=gb[:], in0=gam[:], in1=bi_f[:], op=ALU.mult)
+
+        bo_f = const.tile([P, H], F32, name="bo_f")
+        nc.gpsimd.tensor_scalar(
+            out=bo_f[:], in0=bo_b[:], scalar1=1.0, scalar2=0.0, op0=ALU.mult, op1=ALU.add
+        )
+
+        def codes_pair(nm):
+            cd = keep.tile([P, 2, 512], U32, name=nm + "_c", align_bytes=64)
+            sc = keep.tile([P, 2, 512], U8, name=nm + "_s", align_bytes=64)
+            return cd, sc
+
+        in_q = [codes_pair("inq%d" % c) for c in range(NCH)]
+        wi_q = [codes_pair("wiq%d" % g) for g in range(2)]
+        wo_q = [codes_pair("woq%d" % h) for h in range(2)]
+        x_q = [codes_pair("xq%d" % c) for c in range(NCH)]
+
+        def tq_block(raws, q):
+            stage = stg.tile([P, 2, 512, 2], F32, name="stage", align_bytes=64)
+            for i in range(4):
+                bank = ps_t.tile([P, 2, 2, P], F32, name="bank")
+                words = raws[i].bitcast(F32)
+                for g in range(2):
+                    for u in range(2):
+                        w0 = 256 * g + 128 * u
+                        nc.tensor.transpose(bank[:, g, u, :], words[:, w0 : w0 + 128], ident[:])
+                nc.scalar.copy(
+                    out=stage[:, :, 128 * i : 128 * (i + 1), :],
+                    in_=bank[:].rearrange("p g u c -> p g c u"),
+                )
+            nc.vector.quantize_mx(
+                out=q[0][:].rearrange("p g c -> p (g c)").bitcast(FP8X4),
+                scales=q[1][:].rearrange("p g c -> p (g c)"),
+                in_=stage[:].rearrange("p g c u -> p (g c u)").bitcast(BF16),
+            )
+
+        xs_prev = [None, None]
+
+        def stage1(c, g2):
+            xs = xpool.tile([P, 4, CH], F32, name="xs")
+            first = (c * CH) % SEQ == 0
+            for j in range(4):
+                ct = 4 * g2 + j
+                acc = ps_1.tile([P, CH], F32, name="acc1")
+                for g in range(2):
+                    nc.tensor.matmul_mx(
+                        out=acc[:],
+                        lhsT=wi_q[g2][0][:, g, 128 * j : 128 * (j + 1)].bitcast(FP8X4),
+                        lhsT_scale=wi_q[g2][1][:, g, 128 * j : 128 * (j + 1)],
+                        rhs=in_q[c][0][:, g, :].bitcast(FP8X4),
+                        rhs_scale=in_q[c][1][:, g, :],
+                        start=(g == 0),
+                        stop=(g == 1),
+                    )
+                v = vpool.tile([P, CH], F32, name="v")
+                nc.scalar.activation(
+                    out=v[:],
+                    in_=acc[:],
+                    func=ACTF.Identity,
+                    scale=gam[:, ct : ct + 1],
+                    bias=gb[:, ct : ct + 1],
+                )
+                init = 0.0 if first else xs_prev[g2][:, j, CH - 1 : CH]
+                nc.vector.tensor_tensor_scan(
+                    out=xs[:, j, :],
+                    data0=lam[:, ct : ct + 1].to_broadcast([P, CH]),
+                    data1=v[:],
+                    initial=init,
+                    op0=ALU.mult,
+                    op1=ALU.add,
+                )
+            xs_prev[g2] = xs
+            gx = gpool.tile([P, CH, 4], BF16, name="gx", align_bytes=64)
+            nc.gpsimd.tensor_scalar(
+                out=gx[:],
+                in0=xs[:].rearrange("p j t -> p t j"),
+                scalar1=1.0,
+                scalar2=0.0,
+                op0=ALU.mult,
+                op1=ALU.add,
+            )
+            nc.vector.quantize_mx(
+                out=x_q[c][0][:, g2, :].bitcast(FP8X4),
+                scales=x_q[c][1][:, g2, :],
+                in_=gx[:].rearrange("p t j -> p (t j)"),
+            )
+
+        def stage2(c):
+            for i in range(4):
+                o = opool.tile([P, H], F32, name="o")
+                for h in range(2):
+                    acc = ps_2.tile([P, 512], F32, name="acc2")
+                    for g in range(2):
+                        nc.tensor.matmul_mx(
+                            out=acc[:],
+                            lhsT=x_q[c][0][:, g, 128 * i : 128 * (i + 1)].bitcast(FP8X4),
+                            lhsT_scale=x_q[c][1][:, g, 128 * i : 128 * (i + 1)],
+                            rhs=wo_q[h][0][:, g, :].bitcast(FP8X4),
+                            rhs_scale=wo_q[h][1][:, g, :],
+                            start=(g == 0),
+                            stop=(g == 1),
+                        )
+                    hs = slice(512 * h, 512 * (h + 1))
+                    if h == 1 and i % 2 == 1:
+                        nc.vector.tensor_tensor(out=o[:, hs], in0=acc[:], in1=bo_f[:, hs], op=ALU.add)
+                    else:
+                        nc.scalar.copy(out=o[:, hs], in_=acc[:])
+                        nc.gpsimd.tensor_tensor(out=o[:, hs], in0=o[:, hs], in1=bo_f[:, hs], op=ALU.add)
+                r0 = c * CH + i * P
+                nc.sync.dma_start(out=o_out[r0 : r0 + P, :], in_=o[:])
+
+        def wi_views(g2):
+            return [wi_raw[2 * g2 + u][:, e, :] for u in range(2) for e in range(2)]
+
+        tq_block([in_raw[0][:, i, :] for i in range(4)], in_q[0])
+        tq_block(wi_views(0), wi_q[0])
+        stage1(0, 0)
+        tq_block(wi_views(1), wi_q[1])
+        stage1(0, 1)
+        tq_block([in_raw[1][:, i, :] for i in range(4)], in_q[1])
+        stage1(1, 0)
+        stage1(1, 1)
+        tq_block([wo_raw[0][:, i, :] for i in range(4)], wo_q[0])
+        tq_block([wo_raw[1][:, i, :] for i in range(4)], wo_q[1])
+        stage2(0)
+        tq_block([in_raw[2][:, i, :] for i in range(4)], in_q[2])
+        stage1(2, 0)
+        stage1(2, 1)
+        stage2(1)
+        tq_block([in_raw[3][:, i, :] for i in range(4)], in_q[3])
+        stage1(3, 0)
+        stage1(3, 1)
+        stage2(2)
+        stage2(3)

@@ -39,7 +39,8 @@ def tile_slru_kernel(tc, inputs, Wi, bi, Wo, bo, params_log, out):
         opool = ctx.enter_context(tc.tile_pool(name="op", bufs=4))
         ps_t = ctx.enter_context(tc.psum_pool(name="pst", bufs=2))
         ps_1 = ctx.enter_context(tc.psum_pool(name="ps1", bufs=3))
-        ps_2 = ctx.enter_context(tc.psum_pool(name="ps2", bufs=3))
+        ps_2 = ctx.enter_context(tc.psum_pool(name="ps2", bufs=2))
+        ps_c = ctx.enter_context(tc.psum_pool(name="psc", bufs=1))
 
         in_raw = []
         for c in range(NCH):
@@ -108,6 +109,8 @@ def tile_slru_kernel(tc, inputs, Wi, bi, Wo, bo, params_log, out):
         bi_f = const.tile([P, 8], F32, name="bi_f")
         nc.scalar.activation(out=nu[:], in_=pl[0][:], func=ACTF.Exp)
         nc.scalar.activation(out=lam[:], in_=nu[:], func=ACTF.Exp, scale=-1.0)
+        lam_p = ps_c.tile([P, 8], F32, name="lam_p")
+        nc.tensor.matmul(out=lam_p[:], lhsT=ident[:], rhs=lam[:], start=True, stop=True)
         nc.scalar.activation(out=gam[:], in_=pl[1][:], func=ACTF.Exp)
         nc.vector.tensor_copy(out=bi_f[:], in_=bi_b[:])
         nc.vector.tensor_tensor(out=gb[:], in0=gam[:], in1=bi_f[:], op=ALU.mult)
@@ -175,7 +178,7 @@ def tile_slru_kernel(tc, inputs, Wi, bi, Wo, bo, params_log, out):
                 init = 0.0 if first else xs_prev[g2][:, j, CH - 1 : CH]
                 nc.vector.tensor_tensor_scan(
                     out=xs[:, j, :],
-                    data0=lam[:, ct : ct + 1].to_broadcast([P, CH]),
+                    data0=lam_p[:, ct : ct + 1].to_broadcast([P, CH]),
                     data1=v[:],
                     initial=init,
                     op0=ALU.mult,

from contextlib import ExitStack

import concourse.bass as bass
import concourse.mybir as mybir
import concourse.tile as tile
from concourse.masks import make_identity

F32 = mybir.dt.float32
BF16 = mybir.dt.bfloat16
U32 = mybir.dt.uint32
U8 = mybir.dt.uint8
FP8X4 = mybir.dt.float8_e4m3fn_x4
ACTF = mybir.ActivationFunctionType
ALU = mybir.AluOpType

P = 128
TOK = 2048
SEQ = 1024
H = 1024
U = 1024
CH = 512
NCH = TOK // CH

FLOPS = 2 * 2 * TOK * H * U


def tile_slru_kernel(tc, inputs, Wi, bi, Wo, bo, params_log, out):
    nc = tc.nc
    x_in = inputs.flatten_outer_dims()
    o_out = out.flatten_outer_dims()
    with ExitStack() as ctx:
        const = ctx.enter_context(tc.tile_pool(name="const", bufs=1))
        rawp = ctx.enter_context(tc.tile_pool(name="raw", bufs=1))
        keep = ctx.enter_context(tc.tile_pool(name="keep", bufs=1))
        stg = ctx.enter_context(tc.tile_pool(name="stg", bufs=2))
        vpool = ctx.enter_context(tc.tile_pool(name="vp", bufs=8))
        xpool = ctx.enter_context(tc.tile_pool(name="xp", bufs=4))
        gpool = ctx.enter_context(tc.tile_pool(name="gp", bufs=2))
        opool = ctx.enter_context(tc.tile_pool(name="op", bufs=4))
        ps_t = ctx.enter_context(tc.psum_pool(name="pst", bufs=2))
        ps_1 = ctx.enter_context(tc.psum_pool(name="ps1", bufs=3))
        ps_2 = ctx.enter_context(tc.psum_pool(name="ps2", bufs=2))
        ps_c = ctx.enter_context(tc.psum_pool(name="psc", bufs=1))

        in_raw = []
        for c in range(NCH):
            t = rawp.tile([P, 4, H], BF16, name="in_raw%d" % c)
            in_raw.append(t)
        wi_raw = []
        for a in range(4):
            t = rawp.tile([P, 2, H], BF16, name="wi_raw%d" % a)
            wi_raw.append(t)
        wo_raw = []
        for h in range(2):
            t = rawp.tile([P, 4, U], BF16, name="wo_raw%d" % h)
            wo_raw.append(t)

        pl = [const.tile([P, 8], BF16, name="pl%d" % r) for r in range(2)]
        bi_b = const.tile([P, 8], BF16, name="bi_b")
        for r in range(2):
            nc.scalar.dma_start(
                out=pl[r][:].rearrange("m (a e) -> m a e", e=2),
                in_=params_log[r].rearrange("(a m e) -> m a e", a=4, e=2),
            )
        nc.scalar.dma_start(
            out=bi_b[:].rearrange("m (a e) -> m a e", e=2),
            in_=bi.rearrange("(a m e) -> m a e", a=4, e=2),
        )

        def load_in(c, split):
            src = x_in[c * CH : (c + 1) * CH, :].rearrange("(i p) h -> p i h", p=P)
            if split:
                for i in range(4):
                    nc.sync.dma_start(out=in_raw[c][:, i, :], in_=src[:, i, :])
            else:
                nc.sync.dma_start(out=in_raw[c][:], in_=src)

        def load_wi(a):
            nc.sync.dma_start(
                out=wi_raw[a][:],
                in_=Wi[a * 256 : (a + 1) * 256, :].rearrange("(m e) h -> m e h", e=2),
            )

        def load_wo(h):
            nc.sync.dma_start(
                out=wo_raw[h][:],
                in_=Wo[h * 512 : (h + 1) * 512, :].rearrange("(i p) u -> p i u", p=P),
            )

        load_in(0, True)
        for a in range(4):
            load_wi(a)
        load_in(1, False)
        load_wo(0)
        load_wo(1)
        load_in(2, False)
        load_in(3, False)

        bo_b = const.tile([P, H], BF16, name="bo_b")
        nc.gpsimd.dma_start(out=bo_b[:], in_=bo.partition_broadcast(P))

        ident = const.tile([P, P], F32, name="ident")
        make_identity(nc, ident[:])

        nu = const.tile([P, 8], F32, name="nu")
        lam = const.tile([P, 8], F32, name="lam")
        gam = const.tile([P, 8], F32, name="gam")
        gb = const.tile([P, 8], F32, name="gb")
        bi_f = const.tile([P, 8], F32, name="bi_f")
        nc.scalar.activation(out=nu[:], in_=pl[0][:], func=ACTF.Exp)
        nc.scalar.activation(out=lam[:], in_=nu[:], func=ACTF.Exp, scale=-1.0)
        lam_p = ps_c.tile([P, 8], F32, name="lam_p")
        nc.tensor.matmul(out=lam_p[:], lhsT=ident[:], rhs=lam[:], start=True, stop=True)
        nc.scalar.activation(out=gam[:], in_=pl[1][:], func=ACTF.Exp)
        nc.vector.tensor_copy(out=bi_f[:], in_=bi_b[:])
        nc.vector.tensor_tensor(out=gb[:], in0=gam[:], in1=bi_f[:], op=ALU.mult)

        bo_f = const.tile([P, H], F32, name="bo_f")
        nc.gpsimd.tensor_scalar(
            out=bo_f[:], in0=bo_b[:], scalar1=1.0, scalar2=0.0, op0=ALU.mult, op1=ALU.add
        )

        def codes_pair(nm):
            cd = keep.tile([P, 2, 512], U32, name=nm + "_c", align_bytes=64)
            sc = keep.tile([P, 2, 512], U8, name=nm + "_s", align_bytes=64)
            return cd, sc

        in_q = [codes_pair("inq%d" % c) for c in range(NCH)]
        wi_q = [codes_pair("wiq%d" % g) for g in range(2)]
        wo_q = [codes_pair("woq%d" % h) for h in range(2)]
        x_q = [codes_pair("xq%d" % c) for c in range(NCH)]

        def tq_block(raws, q):
            stage = stg.tile([P, 2, 512, 2], F32, name="stage", align_bytes=64)
            for i in range(4):
                bank = ps_t.tile([P, 2, 2, P], F32, name="bank")
                words = raws[i].bitcast(F32)
                for g in range(2):
                    for u in range(2):
                        w0 = 256 * g + 128 * u
                        nc.tensor.transpose(bank[:, g, u, :], words[:, w0 : w0 + 128], ident[:])
                nc.scalar.copy(
                    out=stage[:, :, 128 * i : 128 * (i + 1), :],
                    in_=bank[:].rearrange("p g u c -> p g c u"),
                )
            nc.vector.quantize_mx(
                out=q[0][:].rearrange("p g c -> p (g c)").bitcast(FP8X4),
                scales=q[1][:].rearrange("p g c -> p (g c)"),
                in_=stage[:].rearrange("p g c u -> p (g c u)").bitcast(BF16),
            )

        xs_prev = [None, None]

        def stage1(c, g2):
            xs = xpool.tile([P, 4, CH], F32, name="xs")
            first = (c * CH) % SEQ == 0
            for j in range(4):
                ct = 4 * g2 + j
                acc = ps_1.tile([P, CH], F32, name="acc1")
                for g in range(2):
                    nc.tensor.matmul_mx(
                        out=acc[:],
                        lhsT=wi_q[g2][0][:, g, 128 * j : 128 * (j + 1)].bitcast(FP8X4),
                        lhsT_scale=wi_q[g2][1][:, g, 128 * j : 128 * (j + 1)],
                        rhs=in_q[c][0][:, g, :].bitcast(FP8X4),
                        rhs_scale=in_q[c][1][:, g, :],
                        start=(g == 0),
                        stop=(g == 1),
                    )
                v = vpool.tile([P, CH], F32, name="v")
                nc.scalar.activation(
                    out=v[:],
                    in_=acc[:],
                    func=ACTF.Identity,
                    scale=gam[:, ct : ct + 1],
                    bias=gb[:, ct : ct + 1],
                )
                init = 0.0 if first else xs_prev[g2][:, j, CH - 1 : CH]
                nc.vector.tensor_tensor_scan(
                    out=xs[:, j, :],
                    data0=lam_p[:, ct : ct + 1].to_broadcast([P, CH]),
                    data1=v[:],
                    initial=init,
                    op0=ALU.mult,
                    op1=ALU.add,
                )
            xs_prev[g2] = xs
            gx = gpool.tile([P, CH, 4], BF16, name="gx", align_bytes=64)
            nc.gpsimd.tensor_scalar(
                out=gx[:],
                in0=xs[:].rearrange("p j t -> p t j"),
                scalar1=1.0,
                scalar2=0.0,
                op0=ALU.mult,
                op1=ALU.add,
            )
            nc.vector.quantize_mx(
                out=x_q[c][0][:, g2, :].bitcast(FP8X4),
                scales=x_q[c][1][:, g2, :],
                in_=gx[:].rearrange("p t j -> p (t j)"),
            )

        def stage2(c):
            for i in range(4):
                o = opool.tile([P, H], F32, name="o")
                for h in range(2):
                    acc = ps_2.tile([P, 512], F32, name="acc2")
                    for g in range(2):
                        nc.tensor.matmul_mx(
                            out=acc[:],
                            lhsT=x_q[c][0][:, g, 128 * i : 128 * (i + 1)].bitcast(FP8X4),
                            lhsT_scale=x_q[c][1][:, g, 128 * i : 128 * (i + 1)],
                            rhs=wo_q[h][0][:, g, :].bitcast(FP8X4),
                            rhs_scale=wo_q[h][1][:, g, :],
                            start=(g == 0),
                            stop=(g == 1),
                        )
                    hs = slice(512 * h, 512 * (h + 1))
                    if h == 1 and i % 2 == 1:
                        nc.vector.tensor_tensor(out=o[:, hs], in0=acc[:], in1=bo_f[:, hs], op=ALU.add)
                    else:
                        nc.scalar.copy(out=o[:, hs], in_=acc[:])
                        nc.gpsimd.tensor_tensor(out=o[:, hs], in0=o[:, hs], in1=bo_f[:, hs], op=ALU.add)
                r0 = c * CH + i * P
                nc.sync.dma_start(out=o_out[r0 : r0 + P, :], in_=o[:])

        def wi_views(g2):
            return [wi_raw[2 * g2 + u][:, e, :] for u in range(2) for e in range(2)]

        tq_block([in_raw[0][:, i, :] for i in range(4)], in_q[0])
        tq_block(wi_views(0), wi_q[0])
        stage1(0, 0)
        tq_block(wi_views(1), wi_q[1])
        stage1(0, 1)
        tq_block([in_raw[1][:, i, :] for i in range(4)], in_q[1])
        stage1(1, 0)
        stage1(1, 1)
        tq_block([wo_raw[0][:, i, :] for i in range(4)], wo_q[0])
        tq_block([wo_raw[1][:, i, :] for i in range(4)], wo_q[1])
        stage2(0)
        tq_block([in_raw[2][:, i, :] for i in range(4)], in_q[2])
        stage1(2, 0)
        stage1(2, 1)
        stage2(1)
        tq_block([in_raw[3][:, i, :] for i in range(4)], in_q[3])
        stage1(3, 0)
        stage1(3, 1)
        stage2(2)
        stage2(3)
